import numpy as np
import ml_dtypes


def mxq(x, axis, fmt="e4m3"):
    dtype, down = {"e4m3": (ml_dtypes.float8_e4m3fn, 7), "e5m2": (ml_dtypes.float8_e5m2, 14)}[fmt]
    v = np.moveaxis(np.asarray(x, np.float32).astype(ml_dtypes.bfloat16).astype(np.float64), axis, -1)
    blocks = v.reshape(v.shape[:-1] + (-1, 32))
    amax = np.abs(blocks).max(-1, keepdims=True)
    byte = np.maximum(np.where(amax > 0, np.frexp(amax)[1] - 1 + 127, 0) - down, 1)
    scale = np.exp2(byte - 127.0)
    codes = (blocks / scale).astype(np.float32).astype(dtype).astype(np.float64)
    return np.moveaxis((codes * scale).reshape(v.shape), -1, axis)


WIDE = False


def mx_kscale(k):
    if not WIDE:
        return np.ones(k)
    levels = np.array([10, -10, 5, -5, 0])
    if k % 512:
        return np.exp2(np.random.permutation(np.resize(levels, k // 32))).repeat(32)
    a = np.empty((k // 512, 16))
    for p in range(k // 512):
        a[p, :8] = np.random.permutation(np.resize(levels, 8))
        for g in range(8):
            far = levels[np.abs(levels - a[p, g]) >= 10]
            a[p, g + 8] = far[np.random.randint(len(far))]
    return np.exp2(a.ravel()).repeat(32)


BF16 = ml_dtypes.bfloat16


def bf(x):
    return np.asarray(x, np.float32).astype(BF16)


def f64(x):
    return np.asarray(x).astype(np.float64)


B, S, DIM, HID, R, NT = 8, 64, 1024, 2560, 128, 3
SCALING = 4.0


def silu(v):
    return v / (1.0 + np.exp(-v))


def lora_out(xa, bw, tw):
    return (xa @ bw) * SCALING * tw[..., None]


def draw0():
    s = mx_kscale(DIM)
    return {"x": bf(np.random.standard_normal((B, S, DIM)) * s),
            "w1": bf(np.random.standard_normal((DIM, HID)) / np.sqrt(DIM) / s[:, None]),
            "w3": bf(np.random.standard_normal((DIM, HID)) / np.sqrt(DIM) / s[:, None]),
            "xa_up": bf(np.random.standard_normal((B, S, R))),
            "b_up": bf(np.random.standard_normal((R, HID)) * 0.2 / np.sqrt(R)),
            "xa_gate": bf(np.random.standard_normal((B, S, R))),
            "b_gate": bf(np.random.standard_normal((R, HID)) * 0.2 / np.sqrt(R)),
            "tw_up": bf(np.random.uniform(size=(B, S))),
            "tw_gate": bf(np.random.uniform(size=(B, S)))}


def core(x, w1, w3, xa_up, b_up, xa_gate, b_gate, tw_up, tw_gate):
    xq = mxq(f64(x), 2, "e4m3")
    up = (xq @ mxq(f64(w3), 0, "e4m3")) + lora_out(f64(xa_up), f64(b_up), f64(tw_up))
    gate = silu((xq @ mxq(f64(w1), 0, "e4m3")) + lora_out(f64(xa_gate), f64(b_gate), f64(tw_gate)))
    return gate * up


def e4m3fn_bytes(y):
    return np.clip(np.asarray(y, np.float64), -448.0, 448.0).astype(np.float32).astype(ml_dtypes.float8_e4m3fn).view(np.uint8)


def e4m3fn_values(b):
    return np.asarray(b, np.uint8).view(ml_dtypes.float8_e4m3fn).astype(np.float64)


def setup_inputs():
    d = draw0()
    x0 = np.asarray(d['w3']).astype(np.float64)
    s = (np.max(np.abs(x0), axis=(1,), keepdims=True) / 448.0).astype(np.float32)
    out = {}
    for k, v in d.items():
        if k == 'w3':
            out['w3_bytes'] = e4m3fn_bytes(x0 / s.astype(np.float64))
            out['w3_scale'] = s
        else:
            out[k] = v
    return out


def reference(x, w1, w3_bytes, w3_scale, xa_up, b_up, xa_gate, b_gate, tw_up, tw_gate):
    return core(x, w1, e4m3fn_values(w3_bytes) * w3_scale.astype(np.float64), xa_up, b_up, xa_gate, b_gate, tw_up, tw_gate)

@@ -1,0 +1,296 @@
+from contextlib import ExitStack
+
+import concourse.mybir as mybir
+from concourse.masks import make_identity
+
+F32 = mybir.dt.float32
+BF16 = mybir.dt.bfloat16
+U32 = mybir.dt.uint32
+U8 = mybir.dt.uint8
+FP8 = mybir.dt.float8_e4m3fn
+FP8X4 = mybir.dt.float8_e4m3fn_x4
+ACT = mybir.ActivationFunctionType
+ALU = mybir.AluOpType
+
+TOK, DIM, HID, RANK = 512, 1024, 2560, 128
+P = 128
+PACK = 4
+G = DIM // (P * PACK)
+MT = TOK // P
+CW = 512
+NCH = HID // CW
+NT = NCH * MT
+NQ = NCH * 4
+FLOPS = 2 * TOK * DIM * HID * 2 + 2 * TOK * RANK * HID * 2
+
+SC = 120
+LEAD = 2
+WL = 1
+RAWB = 3
+
+
+def tile_feedforward_pa_kernel(
+    tc, x, w1, w3_bytes, w3_scale, xa_up, b_up, xa_gate, b_gate, tw_up, tw_gate, out
+):
+    nc = tc.nc
+    x_rows = x.rearrange("b s k -> (b s) k")
+    out_rows = out.rearrange("b s n -> (b s) n")
+    w1_view = w1.rearrange("(g p t) n -> g p t n", p=P, t=PACK)
+    w3_view = w3_bytes.rearrange("(g p t) n -> g p t n", p=P, t=PACK)
+
+    with ExitStack() as ctx:
+        keep = ctx.enter_context(tc.tile_pool(name="keep", bufs=1))
+        raw = ctx.enter_context(tc.tile_pool(name="raw", bufs=RAWB))
+        stage = ctx.enter_context(tc.tile_pool(name="stage", bufs=2))
+        wide = ctx.enter_context(tc.tile_pool(name="wide", bufs=4))
+        lor = ctx.enter_context(tc.tile_pool(name="lor", bufs=4))
+        work = ctx.enter_context(tc.tile_pool(name="work", bufs=3))
+        psum = ctx.enter_context(tc.psum_pool(name="psum", bufs=2))
+
+        w1raw, w3b, bup, bgt = {}, {}, {}, {}
+
+        def load_w3(c, g):
+            if g == 0:
+                w3b[c] = raw.tile([P, G, PACK, CW], U8, name="w3_bytes", tag="w3_bytes")
+            nc.sync.dma_start(out=w3b[c][:, g], in_=w3_view[g, :, :, c * CW : (c + 1) * CW])
+
+        def load_w1(c, g):
+            if g == 0:
+                w1raw[c] = raw.tile([P, G, PACK, CW], BF16, name="w1raw", tag="w1raw")
+            nc.sync.dma_start(out=w1raw[c][:, g], in_=w1_view[g, :, :, c * CW : (c + 1) * CW])
+
+        def load_b(c):
+            bup[c] = keep.tile([P, CW], BF16, name="bup%d" % c)
+            nc.sync.dma_start(out=bup[c][:], in_=b_up[:, c * CW : (c + 1) * CW])
+            bgt[c] = keep.tile([P, CW], BF16, name="bgt%d" % c)
+            nc.sync.dma_start(out=bgt[c][:], in_=b_gate[:, c * CW : (c + 1) * CW])
+
+        load_w1(0, 0)
+        sc = keep.tile([P, G * PACK], F32, name="w3sc")
+        nc.sync.dma_start(
+            out=sc[:].rearrange("p (g t) -> p g t", g=G),
+            in_=w3_scale.rearrange("(g p t) o -> p g (t o)", p=P, t=PACK),
+        )
+        load_w3(0, 0)
+        load_w1(0, 1)
+        load_w3(0, 1)
+        x_raw = []
+        for m in range(MT):
+            xr = keep.tile([P, DIM], BF16, name="x_raw%d" % m)
+            nc.sync.dma_start(out=xr[:], in_=x_rows[m * P : (m + 1) * P, :])
+            x_raw.append(xr)
+        xa_raw = {}
+        for key, src in (("u", xa_up), ("g", xa_gate)):
+            xa_raw[key] = keep.tile([P, MT, RANK], BF16, name="xa_raw_%s" % key)
+            nc.sync.dma_start(
+                out=xa_raw[key][:],
+                in_=src.rearrange("b s r -> (b s) r").rearrange("(m p) r -> p m r", p=P),
+            )
+        tw_raw = keep.tile([P, P], BF16, name="tw_raw")
+        nc.gpsimd.memset(tw_raw[:], 0.0)
+        nc.sync.dma_start(out=tw_raw[0:MT, :], in_=tw_up.rearrange("(m a) s -> m (a s)", a=2))
+        nc.sync.dma_start(out=tw_raw[MT : 2 * MT, :], in_=tw_gate.rearrange("(m a) s -> m (a s)", a=2))
+        load_b(0)
+        for c in range(1, RAWB):
+            load_w3(c, 0)
+            load_w3(c, 1)
+            load_w1(c, 0)
+            load_w1(c, 1)
+            load_b(c)
+        for c in range(RAWB, NCH):
+            load_b(c)
+
+        ident_f = keep.tile([P, P], F32, name="ident_f")
+        make_identity(nc, ident_f[:])
+        ident_b = keep.tile([P, P], BF16, name="ident_b")
+        make_identity(nc, ident_b[:])
+        warm = keep.tile([P, 1], F32, name="warm")
+        nc.gpsimd.memset(warm[:], 0.0)
+        warm2 = keep.tile([P, 1], F32, name="warm2")
+        nc.scalar.activation(out=warm2[:], in_=warm[:], func=ACT.Silu)
+
+        w3w, ilv, codes, planes = {}, {}, {}, {}
+        done = {"widen": 0}
+
+        def widen_upto(n):
+            while done["widen"] < min(n, NCH * G * PACK):
+                j = done["widen"]
+                c, r = divmod(j, G * PACK)
+                g, t = divmod(r, PACK)
+                if t == 0:
+                    w3w[(c, g)] = wide.tile([P, PACK, CW], BF16, name="w3w", tag="w3w")
+                nc.scalar.activation(
+                    out=w3w[(c, g)][:, t, :],
+                    in_=w3b[c][:, g, t, :].bitcast(FP8),
+                    func=ACT.Copy,
+                    scale=sc[:, r : r + 1],
+                )
+                done["widen"] = j + 1
+
+        def interleave(q):
+            c, kind = divmod(q, 4)
+            w, g = divmod(kind, 2)
+            if g == 0:
+                ilv[(w, c)] = stage.tile(
+                    [P, G, CW, PACK], BF16, name="il%d" % w, tag="il%d" % w, align_bytes=64
+                )
+            src = w1raw[c][:, g] if w == 0 else w3w[(c, g)][:]
+            dst = ilv[(w, c)]
+            nc.vector.tensor_copy(
+                out=dst[:, g, SC:, :], in_=src[:, :, SC:].rearrange("p t n -> p n t")
+            )
+            nc.scalar.copy(out=dst[:, g, 0:SC, :], in_=src[:, :, 0:SC].rearrange("p t n -> p n t"))
+
+        def quantise(q):
+            c, kind = divmod(q, 4)
+            w, g = divmod(kind, 2)
+            if g == 0:
+                return
+            codes[(w, c)] = keep.tile([P, G, CW], U32, name="codes%d_%d" % (w, c), align_bytes=64)
+            planes[(w, c)] = keep.tile([P, G, CW], U8, name="planes%d_%d" % (w, c), align_bytes=64)
+            nc.vector.quantize_mx(
+                out=codes[(w, c)][:].rearrange("p g n -> p (g n)").bitcast(FP8X4),
+                scales=planes[(w, c)][:].rearrange("p g n -> p (g n)"),
+                in_=ilv[(w, c)][:].rearrange("p g n t -> p (g n t)"),
+            )
+            if w == 1 and c + RAWB < NCH:
+                load_w3(c + RAWB, 0)
+                load_w3(c + RAWB, 1)
+                load_w1(c + RAWB, 0)
+                load_w1(c + RAWB, 1)
+
+        xt, xg, xc, xs = {}, {}, {}, {}
+
+        def x_turn(m):
+            words = x_raw[m][:].bitcast(F32)
+            tag = "mu" if m % 2 == 0 else "mg"
+            xt[m] = psum.tile([P, G, 2, P], F32, name="xt", tag=tag)
+            for g in range(G):
+                for u in range(2):
+                    nc.tensor.transpose(
+                        xt[m][:, g, u, :], words[:, 256 * g + u : 256 * (g + 1) : 2], ident_f[:]
+                    )
+
+        def x_out(m):
+            xg[m] = stage.tile([P, G * P * PACK], BF16, name="xg", tag="xg", align_bytes=64)
+            nc.vector.tensor_copy(
+                out=xg[m][:].bitcast(F32).rearrange("p (g r u) -> p g r u", g=G, u=2),
+                in_=xt[m][:].rearrange("p g u r -> p g r u"),
+            )
+
+        def x_quant(m):
+            xc[m] = keep.tile([P, G * P], U32, name="xc%d" % m, align_bytes=64)
+            xs[m] = keep.tile([P, G * P], U8, name="xs%d" % m, align_bytes=64)
+            nc.vector.quantize_mx(out=xc[m][:].bitcast(FP8X4), scales=xs[m][:], in_=xg[m][:])
+
+        xaT = {}
+        tw4 = keep.tile([P, 2 * MT], F32, name="tw4")
+
+        def small_operands():
+            for key, tag in (("u", "lu"), ("g", "lg")):
+                ps = psum.tile([P, MT, P], BF16, name="xaT_ps", tag=tag)
+                for m in range(MT):
+                    nc.tensor.transpose(ps[:, m, :], xa_raw[key][:, m, :], ident_b[:])
+                xaT[key] = keep.tile([P, MT, P], BF16, name="xaT_%s" % key)
+                nc.scalar.copy(out=xaT[key][:], in_=ps[:])
+            twT = psum.tile([P, P], BF16, name="twT", tag="lu")
+            nc.tensor.transpose(twT[:], tw_raw[:], ident_b[:])
+            nc.scalar.activation(out=tw4[:], in_=twT[:, 0 : 2 * MT], func=ACT.Copy, scale=4.0)
+
+        lu, lg, mu, mg, a_u, a_g, s_t, u_t = {}, {}, {}, {}, {}, {}, {}, {}
+
+        def lora_mm(i):
+            c, m = divmod(i, MT)
+            lg[i] = psum.tile([P, CW], F32, name="lg", tag="lg")
+            nc.tensor.matmul(lg[i][:], lhsT=xaT["g"][:, m, :], rhs=bgt[c][:], start=True, stop=True)
+            lu[i] = psum.tile([P, CW], F32, name="lu", tag="lu")
+            nc.tensor.matmul(lu[i][:], lhsT=xaT["u"][:, m, :], rhs=bup[c][:], start=True, stop=True)
+
+        def lora_out(i):
+            m = i % MT
+            a_g[i] = lor.tile([P, CW], F32, name="a_g", tag="a_g")
+            nc.scalar.activation(
+                out=a_g[i][:], in_=lg[i][:], func=ACT.Copy, scale=tw4[:, MT + m : MT + m + 1]
+            )
+            a_u[i] = lor.tile([P, CW], F32, name="a_u", tag="a_u")
+            nc.scalar.activation(out=a_u[i][:], in_=lu[i][:], func=ACT.Copy, scale=tw4[:, m : m + 1])
+
+        def mx_mm(i):
+            c, m = divmod(i, MT)
+            mg[i] = psum.tile([P, CW], F32, name="mg", tag="mg")
+            mu[i] = psum.tile([P, CW], F32, name="mu", tag="mu")
+            for w, acc in ((0, mg[i]), (1, mu[i])):
+                for g in range(G):
+                    nc.tensor.matmul_mx(
+                        out=acc[:],
+                        lhsT=xc[m][:, g * P : (g + 1) * P].bitcast(FP8X4),
+                        lhsT_scale=xs[m][:, g * P : (g + 1) * P],
+                        rhs=codes[(w, c)][:, g, :].bitcast(FP8X4),
+                        rhs_scale=planes[(w, c)][:, g, :],
+                        start=(g == 0),
+                        stop=(g == G - 1),
+                    )
+
+        def sums(i):
+            g_t = work.tile([P, CW], F32, name="g_t", tag="g_t")
+            nc.vector.tensor_tensor(out=g_t[:], in0=mg[i][:], in1=a_g[i][:], op=ALU.add)
+            s_t[i] = work.tile([P, CW], F32, name="s_t", tag="s_t")
+            nc.scalar.activation(out=s_t[i][:], in_=g_t[:], func=ACT.Silu)
+            u_t[i] = work.tile([P, CW], F32, name="u_t", tag="u_t")
+            nc.vector.tensor_tensor(out=u_t[i][:], in0=mu[i][:], in1=a_u[i][:], op=ALU.add)
+
+        def product(i):
+            c, m = divmod(i, MT)
+            h_t = work.tile([P, CW], F32, name="h_t", tag="h_t")
+            nc.vector.tensor_tensor(out=h_t[:], in0=u_t[i][:], in1=s_t[i][:], op=ALU.mult)
+            nc.sync.dma_start(
+                out=out_rows[m * P : (m + 1) * P, c * CW : (c + 1) * CW], in_=h_t[:]
+            )
+
+        def piece(q):
+            widen_upto(2 * (q + 1 + WL))
+            interleave(q)
+
+        piece(0)
+        x_turn(0)
+        x_turn(1)
+        x_out(0)
+        x_out(1)
+        piece(1)
+        x_turn(2)
+        x_turn(3)
+        x_quant(0)
+        x_quant(1)
+        x_out(2)
+        x_out(3)
+        quantise(1)
+        small_operands()
+        piece(2)
+        x_quant(2)
+        x_quant(3)
+        piece(3)
+        lora_mm(0)
+        lora_out(0)
+        lora_mm(1)
+        lora_out(1)
+        piece(4)
+        quantise(3)
+        mx_mm(0)
+        piece(5)
+        quantise(5)
+
+        for i in range(NT):
+            q = i + 4 + LEAD
+            if i + 2 < NT:
+                lora_mm(i + 2)
+                lora_out(i + 2)
+            if i + 1 < NT:
+                mx_mm(i + 1)
+            if q < NQ:
+                piece(q)
+            sums(i)
+            if q < NQ:
+                quantise(q)
+            if i > 0:
+                product(i - 1)
+        product(NT - 1)

@@ -23,9 +23,12 @@ NT = NCH * MT
 NQ = NCH * 4
 FLOPS = 2 * TOK * DIM * HID * 2 + 2 * TOK * RANK * HID * 2
 
-SC = 120
-LEAD = 2
-WL = 1
+SC = 48
+GC = 176
+OVER = 4
+NO_G = (0, 3, 4)
+LEAD = 1
+WL = 3
 RAWB = 3
 
 
@@ -46,6 +49,7 @@ def tile_feedforward_pa_kernel(
         lor = ctx.enter_context(tc.tile_pool(name="lor", bufs=4))
         work = ctx.enter_context(tc.tile_pool(name="work", bufs=3))
         psum = ctx.enter_context(tc.psum_pool(name="psum", bufs=2))
+        ctx.enter_context(tc.manual_schedule(engines={mybir.EngineType.DVE}))
 
         w1raw, w3b, bup, bgt = {}, {}, {}, {}
 
@@ -65,20 +69,26 @@ def tile_feedforward_pa_kernel(
             bgt[c] = keep.tile([P, CW], BF16, name="bgt%d" % c)
             nc.sync.dma_start(out=bgt[c][:], in_=b_gate[:, c * CW : (c + 1) * CW])
 
-        load_w1(0, 0)
+        warm = keep.tile([P, 1], F32, name="warm")
+        nc.gpsimd.memset(warm[:], 0.0)
+        warm2 = keep.tile([P, 1], F32, name="warm2")
+        nc.scalar.activation(out=warm2[:], in_=warm[:], func=ACT.Silu)
+
         sc = keep.tile([P, G * PACK], F32, name="w3sc")
         nc.sync.dma_start(
             out=sc[:].rearrange("p (g t) -> p g t", g=G),
             in_=w3_scale.rearrange("(g p t) o -> p g (t o)", p=P, t=PACK),
         )
         load_w3(0, 0)
+        load_w1(0, 0)
         load_w1(0, 1)
-        load_w3(0, 1)
         x_raw = []
         for m in range(MT):
             xr = keep.tile([P, DIM], BF16, name="x_raw%d" % m)
             nc.sync.dma_start(out=xr[:], in_=x_rows[m * P : (m + 1) * P, :])
             x_raw.append(xr)
+            if m == 1:
+                load_w3(0, 1)
         xa_raw = {}
         for key, src in (("u", xa_up), ("g", xa_gate)):
             xa_raw[key] = keep.tile([P, MT, RANK], BF16, name="xa_raw_%s" % key)
@@ -104,10 +114,6 @@ def tile_feedforward_pa_kernel(
         make_identity(nc, ident_f[:])
         ident_b = keep.tile([P, P], BF16, name="ident_b")
         make_identity(nc, ident_b[:])
-        warm = keep.tile([P, 1], F32, name="warm")
-        nc.gpsimd.memset(warm[:], 0.0)
-        warm2 = keep.tile([P, 1], F32, name="warm2")
-        nc.scalar.activation(out=warm2[:], in_=warm[:], func=ACT.Silu)
 
         w3w, ilv, codes, planes = {}, {}, {}, {}
         done = {"widen": 0}
@@ -136,10 +142,22 @@ def tile_feedforward_pa_kernel(
                 )
             src = w1raw[c][:, g] if w == 0 else w3w[(c, g)][:]
             dst = ilv[(w, c)]
+            gc = 0 if q in NO_G else GC
+            v0 = max(gc - OVER, 0)
+            v1 = CW - SC
             nc.vector.tensor_copy(
-                out=dst[:, g, SC:, :], in_=src[:, :, SC:].rearrange("p t n -> p n t")
+                out=dst[:, g, v0:v1, :], in_=src[:, :, v0:v1].rearrange("p t n -> p n t")
             )
-            nc.scalar.copy(out=dst[:, g, 0:SC, :], in_=src[:, :, 0:SC].rearrange("p t n -> p n t"))
+            if gc > 0:
+                nc.gpsimd.tensor_scalar(
+                    out=dst[:, g, 0:gc, :],
+                    in0=src[:, :, 0:gc].rearrange("p t n -> p n t"),
+                    scalar1=1.0,
+                    scalar2=0.0,
+                    op0=ALU.mult,
+                    op1=ALU.add,
+                )
+            nc.scalar.copy(out=dst[:, g, v1:CW, :], in_=src[:, :, v1:CW].rearrange("p t n -> p n t"))
 
         def quantise(q):
             c, kind = divmod(q, 4)
@@ -172,7 +190,7 @@ def tile_feedforward_pa_kernel(
                     )
 
         def x_out(m):
-            xg[m] = stage.tile([P, G * P * PACK], BF16, name="xg", tag="xg", align_bytes=64)
+            xg[m] = stage.tile([P, G * P * PACK], BF16, name="xg", tag="xg", bufs=MT, align_bytes=64)
             nc.vector.tensor_copy(
                 out=xg[m][:].bitcast(F32).rearrange("p (g r u) -> p g r u", g=G, u=2),
                 in_=xt[m][:].rearrange("p g u r -> p g r u"),
@@ -252,22 +270,20 @@ def tile_feedforward_pa_kernel(
             interleave(q)
 
         piece(0)
+        piece(1)
         x_turn(0)
         x_turn(1)
         x_out(0)
         x_out(1)
-        piece(1)
+        piece(2)
         x_turn(2)
         x_turn(3)
-        x_quant(0)
-        x_quant(1)
         x_out(2)
         x_out(3)
         quantise(1)
+        for m in range(MT):
+            x_quant(m)
         small_operands()
-        piece(2)
-        x_quant(2)
-        x_quant(3)
         piece(3)
         lora_mm(0)
         lora_out(0)
@@ -276,8 +292,6 @@ def tile_feedforward_pa_kernel(
         piece(4)
         quantise(3)
         mx_mm(0)
-        piece(5)
-        quantise(5)
 
         for i in range(NT):
             q = i + 4 + LEAD
@@ -289,8 +303,8 @@ def tile_feedforward_pa_kernel(
             if q < NQ:
                 piece(q)
             sums(i)
-            if q < NQ:
-                quantise(q)
             if i > 0:
                 product(i - 1)
+            if q < NQ:
+                quantise(q)
         product(NT - 1)

@@ -23,12 +23,9 @@ NT = NCH * MT
 NQ = NCH * 4
 FLOPS = 2 * TOK * DIM * HID * 2 + 2 * TOK * RANK * HID * 2
 
-SC = 48
-GC = 176
-OVER = 4
-NO_G = (0, 3, 4)
-LEAD = 1
-WL = 3
+SC = 128
+LEAD = 2
+WL = 1
 RAWB = 3
 
 
@@ -49,7 +46,6 @@ def tile_feedforward_pa_kernel(
         lor = ctx.enter_context(tc.tile_pool(name="lor", bufs=4))
         work = ctx.enter_context(tc.tile_pool(name="work", bufs=3))
         psum = ctx.enter_context(tc.psum_pool(name="psum", bufs=2))
-        ctx.enter_context(tc.manual_schedule(engines={mybir.EngineType.DVE}))
 
         w1raw, w3b, bup, bgt = {}, {}, {}, {}
 
@@ -74,21 +70,20 @@ def tile_feedforward_pa_kernel(
         warm2 = keep.tile([P, 1], F32, name="warm2")
         nc.scalar.activation(out=warm2[:], in_=warm[:], func=ACT.Silu)
 
+        load_w1(0, 0)
         sc = keep.tile([P, G * PACK], F32, name="w3sc")
         nc.sync.dma_start(
             out=sc[:].rearrange("p (g t) -> p g t", g=G),
             in_=w3_scale.rearrange("(g p t) o -> p g (t o)", p=P, t=PACK),
         )
         load_w3(0, 0)
-        load_w1(0, 0)
         load_w1(0, 1)
+        load_w3(0, 1)
         x_raw = []
         for m in range(MT):
             xr = keep.tile([P, DIM], BF16, name="x_raw%d" % m)
             nc.sync.dma_start(out=xr[:], in_=x_rows[m * P : (m + 1) * P, :])
             x_raw.append(xr)
-            if m == 1:
-                load_w3(0, 1)
         xa_raw = {}
         for key, src in (("u", xa_up), ("g", xa_gate)):
             xa_raw[key] = keep.tile([P, MT, RANK], BF16, name="xa_raw_%s" % key)
@@ -142,22 +137,18 @@ def tile_feedforward_pa_kernel(
                 )
             src = w1raw[c][:, g] if w == 0 else w3w[(c, g)][:]
             dst = ilv[(w, c)]
-            gc = 0 if q in NO_G else GC
-            v0 = max(gc - OVER, 0)
-            v1 = CW - SC
             nc.vector.tensor_copy(
-                out=dst[:, g, v0:v1, :], in_=src[:, :, v0:v1].rearrange("p t n -> p n t")
+                out=dst[:, g, SC:, :], in_=src[:, :, SC:].rearrange("p t n -> p n t")
             )
-            if gc > 0:
-                nc.gpsimd.tensor_scalar(
-                    out=dst[:, g, 0:gc, :],
-                    in0=src[:, :, 0:gc].rearrange("p t n -> p n t"),
-                    scalar1=1.0,
-                    scalar2=0.0,
-                    op0=ALU.mult,
-                    op1=ALU.add,
-                )
-            nc.scalar.copy(out=dst[:, g, v1:CW, :], in_=src[:, :, v1:CW].rearrange("p t n -> p n t"))
+            ilp = psum.tile([P, SC, PACK], BF16, name="ilp", tag="ilp")
+            nc.tensor.matmul(
+                ilp[:],
+                lhsT=ident_b[:],
+                rhs=src[:, :, 0:SC].rearrange("p t n -> p n t"),
+                start=True,
+                stop=True,
+            )
+            nc.scalar.copy(out=dst[:, g, 0:SC, :], in_=ilp[:])
 
         def quantise(q):
             c, kind = divmod(q, 4)
@@ -190,8 +181,8 @@ def tile_feedforward_pa_kernel(
                     )
 
         def x_out(m):
-            xg[m] = stage.tile([P, G * P * PACK], BF16, name="xg", tag="xg", bufs=MT, align_bytes=64)
-            nc.vector.tensor_copy(
+            xg[m] = stage.tile([P, G * P * PACK], BF16, name="xg", tag="xg", align_bytes=64)
+            nc.scalar.copy(
                 out=xg[m][:].bitcast(F32).rearrange("p (g r u) -> p g r u", g=G, u=2),
                 in_=xt[m][:].rearrange("p g u r -> p g r u"),
             )
@@ -206,12 +197,12 @@ def tile_feedforward_pa_kernel(
 
         def small_operands():
             for key, tag in (("u", "lu"), ("g", "lg")):
-                ps = psum.tile([P, MT, P], BF16, name="xaT_ps", tag=tag)
+                ps = psum.tile([P, MT, P], BF16, name="xaT_ps", tag=tag, bufs=1)
                 for m in range(MT):
                     nc.tensor.transpose(ps[:, m, :], xa_raw[key][:, m, :], ident_b[:])
                 xaT[key] = keep.tile([P, MT, P], BF16, name="xaT_%s" % key)
                 nc.scalar.copy(out=xaT[key][:], in_=ps[:])
-            twT = psum.tile([P, P], BF16, name="twT", tag="lu")
+            twT = psum.tile([P, P], BF16, name="twT", tag="lu", bufs=1)
             nc.tensor.transpose(twT[:], tw_raw[:], ident_b[:])
             nc.scalar.activation(out=tw4[:], in_=twT[:, 0 : 2 * MT], func=ACT.Copy, scale=4.0)
 
@@ -219,9 +210,9 @@ def tile_feedforward_pa_kernel(
 
         def lora_mm(i):
             c, m = divmod(i, MT)
-            lg[i] = psum.tile([P, CW], F32, name="lg", tag="lg")
+            lg[i] = psum.tile([P, CW], F32, name="lg", tag="lg", bufs=1)
             nc.tensor.matmul(lg[i][:], lhsT=xaT["g"][:, m, :], rhs=bgt[c][:], start=True, stop=True)
-            lu[i] = psum.tile([P, CW], F32, name="lu", tag="lu")
+            lu[i] = psum.tile([P, CW], F32, name="lu", tag="lu", bufs=1)
             nc.tensor.matmul(lu[i][:], lhsT=xaT["u"][:, m, :], rhs=bup[c][:], start=True, stop=True)
 
         def lora_out(i):
@@ -249,20 +240,22 @@ def tile_feedforward_pa_kernel(
                         stop=(g == G - 1),
                     )
 
-        def sums(i):
-            g_t = work.tile([P, CW], F32, name="g_t", tag="g_t")
-            nc.vector.tensor_tensor(out=g_t[:], in0=mg[i][:], in1=a_g[i][:], op=ALU.add)
-            s_t[i] = work.tile([P, CW], F32, name="s_t", tag="s_t")
-            nc.scalar.activation(out=s_t[i][:], in_=g_t[:], func=ACT.Silu)
-            u_t[i] = work.tile([P, CW], F32, name="u_t", tag="u_t")
-            nc.vector.tensor_tensor(out=u_t[i][:], in0=mu[i][:], in1=a_u[i][:], op=ALU.add)
+        def sums(i, lo, hi):
+            k = (i, lo)
+            g_t = work.tile([P, hi - lo], F32, name="g_t", tag="g_t")
+            nc.vector.tensor_tensor(out=g_t[:], in0=mg[i][:, lo:hi], in1=a_g[i][:, lo:hi], op=ALU.add)
+            s_t[k] = work.tile([P, hi - lo], F32, name="s_t", tag="s_t")
+            nc.scalar.activation(out=s_t[k][:], in_=g_t[:], func=ACT.Silu)
+            u_t[k] = work.tile([P, hi - lo], F32, name="u_t", tag="u_t")
+            nc.vector.tensor_tensor(out=u_t[k][:], in0=mu[i][:, lo:hi], in1=a_u[i][:, lo:hi], op=ALU.add)
 
-        def product(i):
+        def product(i, lo, hi):
             c, m = divmod(i, MT)
-            h_t = work.tile([P, CW], F32, name="h_t", tag="h_t")
-            nc.vector.tensor_tensor(out=h_t[:], in0=u_t[i][:], in1=s_t[i][:], op=ALU.mult)
+            k = (i, lo)
+            h_t = work.tile([P, hi - lo], F32, name="h_t", tag="h_t")
+            nc.vector.tensor_tensor(out=h_t[:], in0=u_t[k][:], in1=s_t[k][:], op=ALU.mult)
             nc.sync.dma_start(
-                out=out_rows[m * P : (m + 1) * P, c * CW : (c + 1) * CW], in_=h_t[:]
+                out=out_rows[m * P : (m + 1) * P, c * CW + lo : c * CW + hi], in_=h_t[:]
             )
 
         def piece(q):
@@ -270,20 +263,22 @@ def tile_feedforward_pa_kernel(
             interleave(q)
 
         piece(0)
-        piece(1)
         x_turn(0)
         x_turn(1)
         x_out(0)
         x_out(1)
-        piece(2)
+        piece(1)
         x_turn(2)
         x_turn(3)
+        x_quant(0)
+        x_quant(1)
         x_out(2)
         x_out(3)
         quantise(1)
-        for m in range(MT):
-            x_quant(m)
         small_operands()
+        piece(2)
+        x_quant(2)
+        x_quant(3)
         piece(3)
         lora_mm(0)
         lora_out(0)
@@ -292,6 +287,8 @@ def tile_feedforward_pa_kernel(
         piece(4)
         quantise(3)
         mx_mm(0)
+        piece(5)
+        quantise(5)
 
         for i in range(NT):
             q = i + 4 + LEAD
@@ -302,9 +299,14 @@ def tile_feedforward_pa_kernel(
                 mx_mm(i + 1)
             if q < NQ:
                 piece(q)
-            sums(i)
-            if i > 0:
-                product(i - 1)
+            if i < NT - 1:
+                sums(i, 0, CW)
             if q < NQ:
                 quantise(q)
-        product(NT - 1)
+            if i > 0:
+                product(i - 1, 0, CW)
+        half = CW // 2
+        sums(NT - 1, 0, half)
+        sums(NT - 1, half, CW)
+        product(NT - 1, 0, half)
+        product(NT - 1, half, CW)

@@ -24,6 +24,8 @@ NQ = NCH * 4
 FLOPS = 2 * TOK * DIM * HID * 2 + 2 * TOK * RANK * HID * 2
 
 SC = 128
+GC = 104
+GLAP = 4
 LEAD = 2
 WL = 1
 RAWB = 3
@@ -137,9 +139,19 @@ def tile_feedforward_pa_kernel(
                 )
             src = w1raw[c][:, g] if w == 0 else w3w[(c, g)][:]
             dst = ilv[(w, c)]
+            v0 = SC + GC - GLAP if q >= 4 + LEAD else SC
             nc.vector.tensor_copy(
-                out=dst[:, g, SC:, :], in_=src[:, :, SC:].rearrange("p t n -> p n t")
+                out=dst[:, g, v0:, :], in_=src[:, :, v0:].rearrange("p t n -> p n t")
             )
+            if v0 > SC:
+                nc.gpsimd.tensor_scalar(
+                    out=dst[:, g, SC : SC + GC, :],
+                    in0=src[:, :, SC : SC + GC].rearrange("p t n -> p n t"),
+                    scalar1=1.0,
+                    scalar2=0.0,
+                    op0=ALU.mult,
+                    op1=ALU.add,
+                )
             ilp = psum.tile([P, SC, PACK], BF16, name="ilp", tag="ilp")
             nc.tensor.matmul(
                 ilp[:],
@@ -243,11 +255,11 @@ def tile_feedforward_pa_kernel(
         def sums(i, lo, hi):
             k = (i, lo)
             g_t = work.tile([P, hi - lo], F32, name="g_t", tag="g_t")
-            nc.vector.tensor_tensor(out=g_t[:], in0=mg[i][:, lo:hi], in1=a_g[i][:, lo:hi], op=ALU.add)
+            nc.vector.tensor_tensor(out=g_t[:], in0=a_g[i][:, lo:hi], in1=mg[i][:, lo:hi], op=ALU.add)
             s_t[k] = work.tile([P, hi - lo], F32, name="s_t", tag="s_t")
             nc.scalar.activation(out=s_t[k][:], in_=g_t[:], func=ACT.Silu)
             u_t[k] = work.tile([P, hi - lo], F32, name="u_t", tag="u_t")
-            nc.vector.tensor_tensor(out=u_t[k][:], in0=mu[i][:, lo:hi], in1=a_u[i][:, lo:hi], op=ALU.add)
+            nc.vector.tensor_tensor(out=u_t[k][:], in0=a_u[i][:, lo:hi], in1=mu[i][:, lo:hi], op=ALU.add)
 
         def product(i, lo, hi):
             c, m = divmod(i, MT)
@@ -290,6 +302,7 @@ def tile_feedforward_pa_kernel(
         piece(5)
         quantise(5)
 
+        ctx.enter_context(tc.manual_schedule(engines={mybir.EngineType.DVE}))
         for i in range(NT):
             q = i + 4 + LEAD
             if i + 2 < NT:

@@ -302,7 +302,6 @@ def tile_feedforward_pa_kernel(
         piece(5)
         quantise(5)
 
-        ctx.enter_context(tc.manual_schedule(engines={mybir.EngineType.DVE}))
         for i in range(NT):
             q = i + 4 + LEAD
             if i + 2 < NT:

@@ -24,7 +24,7 @@ NQ = NCH * 4
 FLOPS = 2 * TOK * DIM * HID * 2 + 2 * TOK * RANK * HID * 2
 
 SC = 128
-GC = 104
+GC = 108
 GLAP = 4
 LEAD = 2
 WL = 1
@@ -141,7 +141,8 @@ def tile_feedforward_pa_kernel(
             dst = ilv[(w, c)]
             v0 = SC + GC - GLAP if q >= 4 + LEAD else SC
             nc.vector.tensor_copy(
-                out=dst[:, g, v0:, :], in_=src[:, :, v0:].rearrange("p t n -> p n t")
+                out=dst[:, g, v0:, :].rearrange("p (c i) t -> p c t i", i=4),
+                in_=src[:, :, v0:].rearrange("p t (c i) -> p c t i", i=4),
             )
             if v0 > SC:
                 nc.gpsimd.tensor_scalar(

@@ -46,7 +46,7 @@ def tile_feedforward_pa_kernel(
         stage = ctx.enter_context(tc.tile_pool(name="stage", bufs=2))
         wide = ctx.enter_context(tc.tile_pool(name="wide", bufs=4))
         lor = ctx.enter_context(tc.tile_pool(name="lor", bufs=4))
-        work = ctx.enter_context(tc.tile_pool(name="work", bufs=3))
+        work = ctx.enter_context(tc.tile_pool(name="work", bufs=4))
         psum = ctx.enter_context(tc.psum_pool(name="psum", bufs=2))
 
         w1raw, w3b, bup, bgt = {}, {}, {}, {}

@@ -161,7 +161,10 @@ def tile_feedforward_pa_kernel(
                 start=True,
                 stop=True,
             )
-            nc.scalar.copy(out=dst[:, g, 0:SC, :], in_=ilp[:])
+            nc.scalar.copy(
+                out=dst[:, g, 0:SC, :].rearrange("p n t -> p (n t)").bitcast(F32),
+                in_=ilp[:].rearrange("p n t -> p (n t)").bitcast(F32),
+            )
 
         def quantise(q):
             c, kind = divmod(q, 4)

@@ -26,7 +26,7 @@ FLOPS = 2 * TOK * DIM * HID * 2 + 2 * TOK * RANK * HID * 2
 SC = 128
 GC = 108
 GLAP = 4
-LEAD = 2
+LEAD = 3
 WL = 1
 RAWB = 3
 
@@ -305,6 +305,7 @@ def tile_feedforward_pa_kernel(
         mx_mm(0)
         piece(5)
         quantise(5)
+        piece(6)
 
         for i in range(NT):
             q = i + 4 + LEAD

from contextlib import ExitStack

import concourse.mybir as mybir
from concourse.masks import make_identity

F32 = mybir.dt.float32
BF16 = mybir.dt.bfloat16
U32 = mybir.dt.uint32
U8 = mybir.dt.uint8
FP8 = mybir.dt.float8_e4m3fn
FP8X4 = mybir.dt.float8_e4m3fn_x4
ACT = mybir.ActivationFunctionType
ALU = mybir.AluOpType

TOK, DIM, HID, RANK = 512, 1024, 2560, 128
P = 128
PACK = 4
G = DIM // (P * PACK)
MT = TOK // P
CW = 512
NCH = HID // CW
NT = NCH * MT
NQ = NCH * 4
FLOPS = 2 * TOK * DIM * HID * 2 + 2 * TOK * RANK * HID * 2

SC = 128
GC = 108
GLAP = 4
LEAD = 3
WL = 1
RAWB = 3


def tile_feedforward_pa_kernel(
    tc, x, w1, w3_bytes, w3_scale, xa_up, b_up, xa_gate, b_gate, tw_up, tw_gate, out
):
    nc = tc.nc
    x_rows = x.rearrange("b s k -> (b s) k")
    out_rows = out.rearrange("b s n -> (b s) n")
    w1_view = w1.rearrange("(g p t) n -> g p t n", p=P, t=PACK)
    w3_view = w3_bytes.rearrange("(g p t) n -> g p t n", p=P, t=PACK)

    with ExitStack() as ctx:
        keep = ctx.enter_context(tc.tile_pool(name="keep", bufs=1))
        raw = ctx.enter_context(tc.tile_pool(name="raw", bufs=RAWB))
        stage = ctx.enter_context(tc.tile_pool(name="stage", bufs=2))
        wide = ctx.enter_context(tc.tile_pool(name="wide", bufs=4))
        lor = ctx.enter_context(tc.tile_pool(name="lor", bufs=4))
        work = ctx.enter_context(tc.tile_pool(name="work", bufs=4))
        psum = ctx.enter_context(tc.psum_pool(name="psum", bufs=2))

        w1raw, w3b, bup, bgt = {}, {}, {}, {}

        def load_w3(c, g):
            if g == 0:
                w3b[c] = raw.tile([P, G, PACK, CW], U8, name="w3_bytes", tag="w3_bytes")
            nc.sync.dma_start(out=w3b[c][:, g], in_=w3_view[g, :, :, c * CW : (c + 1) * CW])

        def load_w1(c, g):
            if g == 0:
                w1raw[c] = raw.tile([P, G, PACK, CW], BF16, name="w1raw", tag="w1raw")
            nc.sync.dma_start(out=w1raw[c][:, g], in_=w1_view[g, :, :, c * CW : (c + 1) * CW])

        def load_b(c):
            bup[c] = keep.tile([P, CW], BF16, name="bup%d" % c)
            nc.sync.dma_start(out=bup[c][:], in_=b_up[:, c * CW : (c + 1) * CW])
            bgt[c] = keep.tile([P, CW], BF16, name="bgt%d" % c)
            nc.sync.dma_start(out=bgt[c][:], in_=b_gate[:, c * CW : (c + 1) * CW])

        warm = keep.tile([P, 1], F32, name="warm")
        nc.gpsimd.memset(warm[:], 0.0)
        warm2 = keep.tile([P, 1], F32, name="warm2")
        nc.scalar.activation(out=warm2[:], in_=warm[:], func=ACT.Silu)

        load_w1(0, 0)
        sc = keep.tile([P, G * PACK], F32, name="w3sc")
        nc.sync.dma_start(
            out=sc[:].rearrange("p (g t) -> p g t", g=G),
            in_=w3_scale.rearrange("(g p t) o -> p g (t o)", p=P, t=PACK),
        )
        load_w3(0, 0)
        load_w1(0, 1)
        load_w3(0, 1)
        x_raw = []
        for m in range(MT):
            xr = keep.tile([P, DIM], BF16, name="x_raw%d" % m)
            nc.sync.dma_start(out=xr[:], in_=x_rows[m * P : (m + 1) * P, :])
            x_raw.append(xr)
        xa_raw = {}
        for key, src in (("u", xa_up), ("g", xa_gate)):
            xa_raw[key] = keep.tile([P, MT, RANK], BF16, name="xa_raw_%s" % key)
            nc.sync.dma_start(
                out=xa_raw[key][:],
                in_=src.rearrange("b s r -> (b s) r").rearrange("(m p) r -> p m r", p=P),
            )
        tw_raw = keep.tile([P, P], BF16, name="tw_raw")
        nc.gpsimd.memset(tw_raw[:], 0.0)
        nc.sync.dma_start(out=tw_raw[0:MT, :], in_=tw_up.rearrange("(m a) s -> m (a s)", a=2))
        nc.sync.dma_start(out=tw_raw[MT : 2 * MT, :], in_=tw_gate.rearrange("(m a) s -> m (a s)", a=2))
        load_b(0)
        for c in range(1, RAWB):
            load_w3(c, 0)
            load_w3(c, 1)
            load_w1(c, 0)
            load_w1(c, 1)
            load_b(c)
        for c in range(RAWB, NCH):
            load_b(c)

        ident_f = keep.tile([P, P], F32, name="ident_f")
        make_identity(nc, ident_f[:])
        ident_b = keep.tile([P, P], BF16, name="ident_b")
        make_identity(nc, ident_b[:])

        w3w, ilv, codes, planes = {}, {}, {}, {}
        done = {"widen": 0}

        def widen_upto(n):
            while done["widen"] < min(n, NCH * G * PACK):
                j = done["widen"]
                c, r = divmod(j, G * PACK)
                g, t = divmod(r, PACK)
                if t == 0:
                    w3w[(c, g)] = wide.tile([P, PACK, CW], BF16, name="w3w", tag="w3w")
                nc.scalar.activation(
                    out=w3w[(c, g)][:, t, :],
                    in_=w3b[c][:, g, t, :].bitcast(FP8),
                    func=ACT.Copy,
                    scale=sc[:, r : r + 1],
                )
                done["widen"] = j + 1

        def interleave(q):
            c, kind = divmod(q, 4)
            w, g = divmod(kind, 2)
            if g == 0:
                ilv[(w, c)] = stage.tile(
                    [P, G, CW, PACK], BF16, name="il%d" % w, tag="il%d" % w, align_bytes=64
                )
            src = w1raw[c][:, g] if w == 0 else w3w[(c, g)][:]
            dst = ilv[(w, c)]
            v0 = SC + GC - GLAP if q >= 4 + LEAD else SC
            nc.vector.tensor_copy(
                out=dst[:, g, v0:, :].rearrange("p (c i) t -> p c t i", i=4),
                in_=src[:, :, v0:].rearrange("p t (c i) -> p c t i", i=4),
            )
            if v0 > SC:
                nc.gpsimd.tensor_scalar(
                    out=dst[:, g, SC : SC + GC, :],
                    in0=src[:, :, SC : SC + GC].rearrange("p t n -> p n t"),
                    scalar1=1.0,
                    scalar2=0.0,
                    op0=ALU.mult,
                    op1=ALU.add,
                )
            ilp = psum.tile([P, SC, PACK], BF16, name="ilp", tag="ilp")
            nc.tensor.matmul(
                ilp[:],
                lhsT=ident_b[:],
                rhs=src[:, :, 0:SC].rearrange("p t n -> p n t"),
                start=True,
                stop=True,
            )
            nc.scalar.copy(
                out=dst[:, g, 0:SC, :].rearrange("p n t -> p (n t)").bitcast(F32),
                in_=ilp[:].rearrange("p n t -> p (n t)").bitcast(F32),
            )

        def quantise(q):
            c, kind = divmod(q, 4)
            w, g = divmod(kind, 2)
            if g == 0:
                return
            codes[(w, c)] = keep.tile([P, G, CW], U32, name="codes%d_%d" % (w, c), align_bytes=64)
            planes[(w, c)] = keep.tile([P, G, CW], U8, name="planes%d_%d" % (w, c), align_bytes=64)
            nc.vector.quantize_mx(
                out=codes[(w, c)][:].rearrange("p g n -> p (g n)").bitcast(FP8X4),
                scales=planes[(w, c)][:].rearrange("p g n -> p (g n)"),
                in_=ilv[(w, c)][:].rearrange("p g n t -> p (g n t)"),
            )
            if w == 1 and c + RAWB < NCH:
                load_w3(c + RAWB, 0)
                load_w3(c + RAWB, 1)
                load_w1(c + RAWB, 0)
                load_w1(c + RAWB, 1)

        xt, xg, xc, xs = {}, {}, {}, {}

        def x_turn(m):
            words = x_raw[m][:].bitcast(F32)
            tag = "mu" if m % 2 == 0 else "mg"
            xt[m] = psum.tile([P, G, 2, P], F32, name="xt", tag=tag)
            for g in range(G):
                for u in range(2):
                    nc.tensor.transpose(
                        xt[m][:, g, u, :], words[:, 256 * g + u : 256 * (g + 1) : 2], ident_f[:]
                    )

        def x_out(m):
            xg[m] = stage.tile([P, G * P * PACK], BF16, name="xg", tag="xg", align_bytes=64)
            nc.scalar.copy(
                out=xg[m][:].bitcast(F32).rearrange("p (g r u) -> p g r u", g=G, u=2),
                in_=xt[m][:].rearrange("p g u r -> p g r u"),
            )

        def x_quant(m):
            xc[m] = keep.tile([P, G * P], U32, name="xc%d" % m, align_bytes=64)
            xs[m] = keep.tile([P, G * P], U8, name="xs%d" % m, align_bytes=64)
            nc.vector.quantize_mx(out=xc[m][:].bitcast(FP8X4), scales=xs[m][:], in_=xg[m][:])

        xaT = {}
        tw4 = keep.tile([P, 2 * MT], F32, name="tw4")

        def small_operands():
            for key, tag in (("u", "lu"), ("g", "lg")):
                ps = psum.tile([P, MT, P], BF16, name="xaT_ps", tag=tag, bufs=1)
                for m in range(MT):
                    nc.tensor.transpose(ps[:, m, :], xa_raw[key][:, m, :], ident_b[:])
                xaT[key] = keep.tile([P, MT, P], BF16, name="xaT_%s" % key)
                nc.scalar.copy(out=xaT[key][:], in_=ps[:])
            twT = psum.tile([P, P], BF16, name="twT", tag="lu", bufs=1)
            nc.tensor.transpose(twT[:], tw_raw[:], ident_b[:])
            nc.scalar.activation(out=tw4[:], in_=twT[:, 0 : 2 * MT], func=ACT.Copy, scale=4.0)

        lu, lg, mu, mg, a_u, a_g, s_t, u_t = {}, {}, {}, {}, {}, {}, {}, {}

        def lora_mm(i):
            c, m = divmod(i, MT)
            lg[i] = psum.tile([P, CW], F32, name="lg", tag="lg", bufs=1)
            nc.tensor.matmul(lg[i][:], lhsT=xaT["g"][:, m, :], rhs=bgt[c][:], start=True, stop=True)
            lu[i] = psum.tile([P, CW], F32, name="lu", tag="lu", bufs=1)
            nc.tensor.matmul(lu[i][:], lhsT=xaT["u"][:, m, :], rhs=bup[c][:], start=True, stop=True)

        def lora_out(i):
            m = i % MT
            a_g[i] = lor.tile([P, CW], F32, name="a_g", tag="a_g")
            nc.scalar.activation(
                out=a_g[i][:], in_=lg[i][:], func=ACT.Copy, scale=tw4[:, MT + m : MT + m + 1]
            )
            a_u[i] = lor.tile([P, CW], F32, name="a_u", tag="a_u")
            nc.scalar.activation(out=a_u[i][:], in_=lu[i][:], func=ACT.Copy, scale=tw4[:, m : m + 1])

        def mx_mm(i):
            c, m = divmod(i, MT)
            mg[i] = psum.tile([P, CW], F32, name="mg", tag="mg")
            mu[i] = psum.tile([P, CW], F32, name="mu", tag="mu")
            for w, acc in ((0, mg[i]), (1, mu[i])):
                for g in range(G):
                    nc.tensor.matmul_mx(
                        out=acc[:],
                        lhsT=xc[m][:, g * P : (g + 1) * P].bitcast(FP8X4),
                        lhsT_scale=xs[m][:, g * P : (g + 1) * P],
                        rhs=codes[(w, c)][:, g, :].bitcast(FP8X4),
                        rhs_scale=planes[(w, c)][:, g, :],
                        start=(g == 0),
                        stop=(g == G - 1),
                    )

        def sums(i, lo, hi):
            k = (i, lo)
            g_t = work.tile([P, hi - lo], F32, name="g_t", tag="g_t")
            nc.vector.tensor_tensor(out=g_t[:], in0=a_g[i][:, lo:hi], in1=mg[i][:, lo:hi], op=ALU.add)
            s_t[k] = work.tile([P, hi - lo], F32, name="s_t", tag="s_t")
            nc.scalar.activation(out=s_t[k][:], in_=g_t[:], func=ACT.Silu)
            u_t[k] = work.tile([P, hi - lo], F32, name="u_t", tag="u_t")
            nc.vector.tensor_tensor(out=u_t[k][:], in0=a_u[i][:, lo:hi], in1=mu[i][:, lo:hi], op=ALU.add)

        def product(i, lo, hi):
            c, m = divmod(i, MT)
            k = (i, lo)
            h_t = work.tile([P, hi - lo], F32, name="h_t", tag="h_t")
            nc.vector.tensor_tensor(out=h_t[:], in0=u_t[k][:], in1=s_t[k][:], op=ALU.mult)
            nc.sync.dma_start(
                out=out_rows[m * P : (m + 1) * P, c * CW + lo : c * CW + hi], in_=h_t[:]
            )

        def piece(q):
            widen_upto(2 * (q + 1 + WL))
            interleave(q)

        piece(0)
        x_turn(0)
        x_turn(1)
        x_out(0)
        x_out(1)
        piece(1)
        x_turn(2)
        x_turn(3)
        x_quant(0)
        x_quant(1)
        x_out(2)
        x_out(3)
        quantise(1)
        small_operands()
        piece(2)
        x_quant(2)
        x_quant(3)
        piece(3)
        lora_mm(0)
        lora_out(0)
        lora_mm(1)
        lora_out(1)
        piece(4)
        quantise(3)
        mx_mm(0)
        piece(5)
        quantise(5)
        piece(6)

        for i in range(NT):
            q = i + 4 + LEAD
            if i + 2 < NT:
                lora_mm(i + 2)
                lora_out(i + 2)
            if i + 1 < NT:
                mx_mm(i + 1)
            if q < NQ:
                piece(q)
            if i < NT - 1:
                sums(i, 0, CW)
            if q < NQ:
                quantise(q)
            if i > 0:
                product(i - 1, 0, CW)
        half = CW // 2
        sums(NT - 1, 0, half)
        sums(NT - 1, half, CW)
        product(NT - 1, 0, half)
        product(NT - 1, half, CW)
